import numpy as np
import ml_dtypes


def mxq(x, axis, fmt="e4m3"):
    dtype, down = {"e4m3": (ml_dtypes.float8_e4m3fn, 7), "e5m2": (ml_dtypes.float8_e5m2, 14)}[fmt]
    v = np.moveaxis(np.asarray(x, np.float32).astype(ml_dtypes.bfloat16).astype(np.float64), axis, -1)
    blocks = v.reshape(v.shape[:-1] + (-1, 32))
    amax = np.abs(blocks).max(-1, keepdims=True)
    byte = np.maximum(np.where(amax > 0, np.frexp(amax)[1] - 1 + 127, 0) - down, 1)
    scale = np.exp2(byte - 127.0)
    codes = (blocks / scale).astype(np.float32).astype(dtype).astype(np.float64)
    return np.moveaxis((codes * scale).reshape(v.shape), -1, axis)


WIDE = False


def mx_kscale(k):
    if not WIDE:
        return np.ones(k)
    levels = np.array([10, -10, 5, -5, 0])
    a = np.random.permutation(np.resize(levels, k // 512 * 4)).reshape(k // 512, 4)
    idx = np.arange(k)
    return np.exp2(a[idx // 512, idx % 128 // 32])


BF16 = ml_dtypes.bfloat16


def bf(x):
    return np.asarray(x, np.float32).astype(BF16)


def f64(x):
    return np.asarray(x).astype(np.float64)


B, T, D, H, HKV, HD, R, DFF = 1, 128, 512, 16, 8, 64, 128, 6144
HALF = HD // 2
EPS = 1e-6
THETA = 1e6


def rms_norm(x, w):
    return x / np.sqrt(np.mean(x * x, axis=-1, keepdims=True) + EPS) * w


def rotate_half(x):
    return np.concatenate([-x[..., HALF:], x[..., :HALF]], axis=-1)


def setup_inputs():
    rn = np.random.standard_normal
    s = mx_kscale(D)
    inv_freq = 1.0 / THETA ** (np.arange(HALF) / HALF)
    freqs = np.arange(T)[:, None] * inv_freq[None, :]
    emb = np.concatenate([freqs, freqs], axis=-1)
    return {
        "hidden_states": bf(rn((B, T, D)) * np.exp(0.5 * rn((B, T, 1)))),
        "ln1_w": bf((1.0 + 0.1 * rn(D)) * s),
        "Wq": bf(rn((D, H * HD)) / np.sqrt(D) / s[:, None]),
        "Wk": bf(rn((D, HKV * HD)) / np.sqrt(D) / s[:, None]),
        "Wv": bf(rn((D, HKV * HD)) / np.sqrt(D) / s[:, None]),
        "q_norm_w": bf(1.0 + 0.1 * rn(HD)),
        "k_norm_w": bf(1.0 + 0.1 * rn(HD)),
        "cos": bf(np.cos(emb)),
        "sin": bf(np.sin(emb)),
    }


def reference(hidden_states, ln1_w, Wq, Wk, Wv, q_norm_w, k_norm_w, cos, sin):
    h = rms_norm(f64(hidden_states), f64(ln1_w))
    hq = mxq(h, 2, "e4m3")
    q = rms_norm((hq @ mxq(f64(Wq), 0, "e4m3")).reshape(B, T, H, HD), f64(q_norm_w)).transpose(0, 2, 1, 3)
    k = rms_norm((hq @ mxq(f64(Wk), 0, "e4m3")).reshape(B, T, HKV, HD), f64(k_norm_w)).transpose(0, 2, 1, 3)
    v = (hq @ mxq(f64(Wv), 0, "e4m3")).reshape(B, T, HKV, HD).transpose(0, 2, 1, 3)
    c, s_ = f64(cos)[None, None], f64(sin)[None, None]
    q = q * c + rotate_half(q) * s_
    k = k * c + rotate_half(k) * s_
    return q, k, v

@@ -1,0 +1,264 @@
+import concourse.mybir as mybir
+from concourse.masks import make_identity
+
+F32 = mybir.dt.float32
+BF16 = mybir.dt.bfloat16
+U32 = mybir.dt.uint32
+U8 = mybir.dt.uint8
+FP8X4 = mybir.dt.float8_e4m3fn_x4
+ALU = mybir.AluOpType
+ACT = mybir.ActivationFunctionType
+
+P = 128
+PACK = 4
+D = P * PACK
+HD = 64
+HALF = HD // 2
+CHUNK = 512
+HEADS = CHUNK // HD
+EPS = 1e-6
+SCALAR_COLS = 160
+
+FLOPS = 2 * P * D * 4 * CHUNK
+
+
+def tile_rawkvinjector_pa_s_kernel(
+    tc, hidden_states, ln1_w, Wq, Wk, Wv, q_norm_w, k_norm_w, cos, sin, out_0, out_1, out_2
+):
+    nc = tc.nc
+    vector_cols = (0, CHUNK - SCALAR_COLS)
+    scalar_cols = (CHUNK - SCALAR_COLS, CHUNK)
+    chunks = [
+        (Wq, 0, out_0, 0, 0),
+        (Wq, CHUNK, out_0, HEADS, 0),
+        (Wk, 0, out_1, 0, 1),
+        (Wv, 0, out_2, 0, None),
+    ]
+    with (
+        nc.allow_non_contiguous_dma(reason="outputs are stored head by head, 256 bytes a run"),
+        tc.tile_pool(name="keep", bufs=1) as keep,
+        tc.psum_pool(name="psum", bufs=1) as psum,
+        tc.manual_schedule(),
+    ):
+        raw = [keep.tile([P, PACK, CHUNK], BF16, name="raw%d" % c) for c in range(4)]
+        grouped = [
+            keep.tile([P, CHUNK, PACK], BF16, name="grouped%d" % c, align_bytes=64) for c in range(4)
+        ]
+        codes = [keep.tile([P, CHUNK], U32, name="codes%d" % c, align_bytes=64) for c in range(4)]
+        scales = [keep.tile([P, CHUNK], U8, name="scales%d" % c, align_bytes=64) for c in range(4)]
+        prod = [psum.tile([P, HEADS, HD], F32, name="prod%d" % c) for c in range(4)]
+        squares = [keep.tile([P, HEADS, HD], F32, name="squares%d" % c) for c in range(3)]
+        ssq = [keep.tile([P, HEADS], F32, name="ssq%d" % c) for c in range(3)]
+        rstd = [keep.tile([P, HEADS], F32, name="rstd%d" % c) for c in range(3)]
+        normed = [keep.tile([P, HEADS, HD], F32, name="normed%d" % c) for c in range(3)]
+        turned = [keep.tile([P, HEADS, HD], F32, name="turned%d" % c) for c in range(3)]
+        result = [keep.tile([P, HEADS, HD], F32, name="result%d" % c) for c in range(4)]
+        h_codes = keep.tile([P, P], U32, align_bytes=64)
+        h_scales = keep.tile([P, P], U8, align_bytes=64)
+        rope_cos = keep.tile([P, 2, HD], F32)
+        rope_sin = keep.tile([P, 2, HD], F32)
+
+        def load(c, cols):
+            w, col0 = chunks[c][0], chunks[c][1]
+            lo, hi = cols
+            nc.sync.dma_start(
+                out=raw[c][:, :, lo:hi],
+                in_=w.rearrange("(p j) n -> p j n", j=PACK)[:, :, col0 + lo : col0 + hi],
+            )
+
+        def regroup(copy, c, cols):
+            lo, hi = cols
+            copy(
+                out=grouped[c][:, lo:hi, :].rearrange("p (n i) j -> p n j i", i=4),
+                in_=raw[c][:, :, lo:hi].rearrange("p j (n i) -> p n j i", i=4),
+            )
+
+        def quantise(c):
+            nc.vector.quantize_mx(
+                out=codes[c][:].bitcast(FP8X4),
+                scales=scales[c][:],
+                in_=grouped[c][:].rearrange("p n j -> p (n j)"),
+            )
+
+        def multiply(c):
+            nc.tensor.matmul_mx(
+                out=prod[c][:].rearrange("p h d -> p (h d)"),
+                lhsT=h_codes[:].bitcast(FP8X4),
+                lhsT_scale=h_scales[:],
+                rhs=codes[c][:].bitcast(FP8X4),
+                rhs_scale=scales[c][:],
+                start=True,
+                stop=True,
+            )
+
+        def normalise(c, h0, h1):
+            for h in range(h0, h1):
+                nc.scalar.activation(
+                    out=squares[c][:, h, :],
+                    in_=prod[c][:, h, :],
+                    func=ACT.Square,
+                    accum_out=ssq[c][:, h : h + 1],
+                )
+            nc.scalar.activation(
+                out=rstd[c][:, h0:h1],
+                in_=ssq[c][:, h0:h1],
+                func=ACT.Abs_reciprocal_sqrt,
+                scale=1.0 / HD,
+                bias=EPS,
+            )
+            for h in range(h0, h1):
+                nc.scalar.activation(
+                    out=normed[c][:, h, :],
+                    in_=prod[c][:, h, :],
+                    func=ACT.Copy,
+                    scale=rstd[c][:, h : h + 1],
+                )
+
+        def rope(c, h0, h1):
+            norm = chunks[c][4]
+            n = h1 - h0
+            nc.vector.tensor_tensor(
+                out=turned[c][:, h0:h1, 0:HALF],
+                in0=normed[c][:, h0:h1, HALF:HD],
+                in1=rope_sin[:, norm, 0:HALF].unsqueeze(1).to_broadcast([P, n, HALF]),
+                op=ALU.mult,
+            )
+            nc.vector.tensor_tensor(
+                out=turned[c][:, h0:h1, HALF:HD],
+                in0=normed[c][:, h0:h1, 0:HALF],
+                in1=rope_sin[:, norm, HALF:HD].unsqueeze(1).to_broadcast([P, n, HALF]),
+                op=ALU.mult,
+            )
+            nc.vector.tensor_tensor(
+                out=result[c][:, h0:h1, :],
+                in0=normed[c][:, h0:h1, :],
+                in1=rope_cos[:, norm, :].unsqueeze(1).to_broadcast([P, n, HD]),
+                op=ALU.mult,
+            )
+            nc.vector.tensor_tensor(
+                out=result[c][:, h0:h1, :],
+                in0=result[c][:, h0:h1, :],
+                in1=turned[c][:, h0:h1, :],
+                op=ALU.add,
+            )
+
+        def store(c, h0, h1):
+            out, head0 = chunks[c][2], chunks[c][3]
+            nc.sync.dma_start(
+                out=out.rearrange("b h t d -> t (b h) d")[:, head0 + h0 : head0 + h1, :],
+                in_=result[c][:, h0:h1, :],
+            )
+
+        rows = keep.tile([P, D + 2 * HD], BF16)
+        nc.vector.memset(rows[:], 0.0)
+        nc.scalar.dma_start(out=rows[0:1, 0:D], in_=ln1_w.unsqueeze(0))
+        nc.scalar.dma_start(out=rows[0:1, D : D + HD], in_=q_norm_w.unsqueeze(0))
+        nc.scalar.dma_start(out=rows[0:1, D + HD : D + 2 * HD], in_=k_norm_w.unsqueeze(0))
+        x = keep.tile([P, D], BF16)
+        nc.sync.dma_start(out=x[:], in_=hidden_states.rearrange("b t d -> (b t) d"))
+        load(0, vector_cols)
+        load(0, scalar_cols)
+        for c in range(1, 4):
+            load(c, (0, CHUNK))
+        cos_sb = keep.tile([P, HD], BF16)
+        nc.sync.dma_start(out=cos_sb[:], in_=cos)
+        sin_sb = keep.tile([P, HD], BF16)
+        nc.sync.dma_start(out=sin_sb[:], in_=sin)
+
+        ones = keep.tile([P, P], BF16)
+        nc.vector.memset(ones[:], 1.0)
+        ident = keep.tile([P, P], BF16)
+        make_identity(nc, ident[:])
+        warm = keep.tile([P, 1], F32)
+        nc.vector.memset(warm[:], 1.0)
+        nc.scalar.activation(out=warm[:], in_=warm[:], func=ACT.Abs_reciprocal_sqrt)
+
+        ln_bc = psum.tile([P, D], F32)
+        nc.tensor.matmul(out=ln_bc[:], lhsT=ones[:], rhs=rows[:, 0:D], start=True, stop=True)
+        x_sq = keep.tile([P, D], BF16)
+        x_ssq = keep.tile([P, 1], F32)
+        nc.scalar.activation(out=x_sq[:], in_=x[:], func=ACT.Square, accum_out=x_ssq[:])
+        x_rstd = keep.tile([P, 1], F32)
+        nc.scalar.activation(
+            out=x_rstd[:], in_=x_ssq[:], func=ACT.Abs_reciprocal_sqrt, scale=1.0 / D, bias=EPS
+        )
+        regroup(nc.vector.tensor_copy, 0, vector_cols)
+        regroup(nc.scalar.copy, 0, scalar_cols)
+        h_rows = keep.tile([P, PACK, P], BF16)
+        nc.vector.scalar_tensor_tensor(
+            out=h_rows[:],
+            in0=x[:].rearrange("t (p j) -> t j p", j=PACK),
+            scalar=x_rstd[:],
+            in1=ln_bc[:].rearrange("t (p j) -> t j p", j=PACK),
+            op0=ALU.mult,
+            op1=ALU.mult,
+        )
+        hT = psum.tile([P, PACK, P], BF16)
+        for j in range(PACK):
+            nc.tensor.transpose(hT[:, j, :], h_rows[:, j, :], ident[:])
+        h_grouped = keep.tile([P, P, PACK], BF16, align_bytes=64)
+        nc.scalar.copy(out=h_grouped[:], in_=hT[:].rearrange("p j t -> p t j"))
+        regroup(nc.vector.tensor_copy, 1, vector_cols)
+        regroup(nc.scalar.copy, 1, scalar_cols)
+        quantise(0)
+        nc.vector.quantize_mx(
+            out=h_codes[:].bitcast(FP8X4),
+            scales=h_scales[:],
+            in_=h_grouped[:].rearrange("p t j -> p (t j)"),
+        )
+        multiply(0)
+
+        quantise(1)
+        multiply(1)
+        regroup(nc.vector.tensor_copy, 2, vector_cols)
+        regroup(nc.scalar.copy, 2, scalar_cols)
+        regroup(nc.vector.tensor_copy, 3, vector_cols)
+        regroup(nc.scalar.copy, 3, scalar_cols)
+        quantise(2)
+        multiply(2)
+        quantise(3)
+        multiply(3)
+
+        nw_bc = psum.tile([P, 2, HD], F32)
+        nc.tensor.matmul(
+            out=nw_bc[:].rearrange("p g d -> p (g d)"),
+            lhsT=ones[:],
+            rhs=rows[:, D : D + 2 * HD],
+            start=True,
+            stop=True,
+        )
+        nc.vector.tensor_tensor(
+            out=rope_cos[:],
+            in0=nw_bc[:],
+            in1=cos_sb[:].unsqueeze(1).to_broadcast([P, 2, HD]),
+            op=ALU.mult,
+        )
+        nc.vector.scalar_tensor_tensor(
+            out=rope_sin[:, :, 0:HALF],
+            in0=nw_bc[:, :, HALF:HD],
+            scalar=-1.0,
+            in1=sin_sb[:, 0:HALF].unsqueeze(1).to_broadcast([P, 2, HALF]),
+            op0=ALU.mult,
+            op1=ALU.mult,
+        )
+        nc.vector.tensor_tensor(
+            out=rope_sin[:, :, HALF:HD],
+            in0=nw_bc[:, :, 0:HALF],
+            in1=sin_sb[:, HALF:HD].unsqueeze(1).to_broadcast([P, 2, HALF]),
+            op=ALU.mult,
+        )
+
+        normalise(0, 0, HEADS)
+        rope(0, 0, HEADS)
+        store(0, 0, HEADS)
+        normalise(1, 0, HEADS)
+        rope(1, 0, HEADS)
+        store(1, 0, HEADS)
+        normalise(2, 0, HEADS // 2)
+        rope(2, 0, HEADS // 2)
+        store(2, 0, HEADS // 2)
+        normalise(2, HEADS // 2, HEADS)
+        rope(2, HEADS // 2, HEADS)
+        store(2, HEADS // 2, HEADS)
+        nc.scalar.copy(out=result[3][:], in_=prod[3][:])
+        store(3, 0, HEADS)

@@ -17,7 +17,7 @@ HALF = HD // 2
 CHUNK = 512
 HEADS = CHUNK // HD
 EPS = 1e-6
-SCALAR_COLS = 160
+SCALAR_COLS = 256
 
 FLOPS = 2 * P * D * 4 * CHUNK
 
@@ -149,13 +149,10 @@ def tile_rawkvinjector_pa_s_kernel(
                 in_=result[c][:, h0:h1, :],
             )
 
-        rows = keep.tile([P, D + 2 * HD], BF16)
-        nc.vector.memset(rows[:], 0.0)
-        nc.scalar.dma_start(out=rows[0:1, 0:D], in_=ln1_w.unsqueeze(0))
-        nc.scalar.dma_start(out=rows[0:1, D : D + HD], in_=q_norm_w.unsqueeze(0))
-        nc.scalar.dma_start(out=rows[0:1, D + HD : D + 2 * HD], in_=k_norm_w.unsqueeze(0))
         x = keep.tile([P, D], BF16)
         nc.sync.dma_start(out=x[:], in_=hidden_states.rearrange("b t d -> (b t) d"))
+        ln_w = keep.tile([P, PACK], BF16)
+        nc.sync.dma_start(out=ln_w[:], in_=ln1_w.rearrange("(p j) -> p j", j=PACK))
         load(0, vector_cols)
         load(0, scalar_cols)
         for c in range(1, 4):
@@ -164,17 +161,43 @@ def tile_rawkvinjector_pa_s_kernel(
         nc.sync.dma_start(out=cos_sb[:], in_=cos)
         sin_sb = keep.tile([P, HD], BF16)
         nc.sync.dma_start(out=sin_sb[:], in_=sin)
+        norm_w = keep.tile([P, 2, HD], BF16)
+        nc.sync.dma_start(out=norm_w[:, 0, :], in_=q_norm_w.partition_broadcast(P))
+        nc.sync.dma_start(out=norm_w[:, 1, :], in_=k_norm_w.partition_broadcast(P))
 
-        ones = keep.tile([P, P], BF16)
-        nc.vector.memset(ones[:], 1.0)
-        ident = keep.tile([P, P], BF16)
+        ident = keep.tile([P, P], F32)
         make_identity(nc, ident[:])
         warm = keep.tile([P, 1], F32)
         nc.vector.memset(warm[:], 1.0)
         nc.scalar.activation(out=warm[:], in_=warm[:], func=ACT.Abs_reciprocal_sqrt)
 
-        ln_bc = psum.tile([P, D], F32)
-        nc.tensor.matmul(out=ln_bc[:], lhsT=ones[:], rhs=rows[:, 0:D], start=True, stop=True)
+        nc.gpsimd.tensor_tensor(
+            out=rope_cos[:],
+            in0=norm_w[:],
+            in1=cos_sb[:].unsqueeze(1).to_broadcast([P, 2, HD]),
+            op=ALU.mult,
+        )
+        nc.gpsimd.tensor_tensor(
+            out=rope_sin[:, :, HALF:HD],
+            in0=norm_w[:, :, 0:HALF],
+            in1=sin_sb[:, HALF:HD].unsqueeze(1).to_broadcast([P, 2, HALF]),
+            op=ALU.mult,
+        )
+        nc.gpsimd.tensor_tensor(
+            out=rope_sin[:, :, 0:HALF],
+            in0=norm_w[:, :, HALF:HD],
+            in1=sin_sb[:, 0:HALF].unsqueeze(1).to_broadcast([P, 2, HALF]),
+            op=ALU.mult,
+        )
+        nc.gpsimd.tensor_scalar(
+            out=rope_sin[:, :, 0:HALF],
+            in0=rope_sin[:, :, 0:HALF],
+            scalar1=-1.0,
+            scalar2=0.0,
+            op0=ALU.mult,
+            op1=ALU.add,
+        )
+
         x_sq = keep.tile([P, D], BF16)
         x_ssq = keep.tile([P, 1], F32)
         nc.scalar.activation(out=x_sq[:], in_=x[:], func=ACT.Square, accum_out=x_ssq[:])
@@ -184,22 +207,26 @@ def tile_rawkvinjector_pa_s_kernel(
         )
         regroup(nc.vector.tensor_copy, 0, vector_cols)
         regroup(nc.scalar.copy, 0, scalar_cols)
-        h_rows = keep.tile([P, PACK, P], BF16)
-        nc.vector.scalar_tensor_tensor(
-            out=h_rows[:],
+        x_normed = keep.tile([P, PACK, P], F32)
+        nc.vector.tensor_scalar(
+            out=x_normed[:],
             in0=x[:].rearrange("t (p j) -> t j p", j=PACK),
-            scalar=x_rstd[:],
-            in1=ln_bc[:].rearrange("t (p j) -> t j p", j=PACK),
+            scalar1=x_rstd[:],
+            scalar2=None,
             op0=ALU.mult,
-            op1=ALU.mult,
         )
-        hT = psum.tile([P, PACK, P], BF16)
+        x_turned = psum.tile([P, PACK, P], F32)
         for j in range(PACK):
-            nc.tensor.transpose(hT[:, j, :], h_rows[:, j, :], ident[:])
-        h_grouped = keep.tile([P, P, PACK], BF16, align_bytes=64)
-        nc.scalar.copy(out=h_grouped[:], in_=hT[:].rearrange("p j t -> p t j"))
+            nc.tensor.transpose(x_turned[:, j, :], x_normed[:, j, :], ident[:])
         regroup(nc.vector.tensor_copy, 1, vector_cols)
         regroup(nc.scalar.copy, 1, scalar_cols)
+        h_grouped = keep.tile([P, P, PACK], BF16, align_bytes=64)
+        nc.vector.tensor_tensor(
+            out=h_grouped[:],
+            in0=x_turned[:].rearrange("p j t -> p t j"),
+            in1=ln_w[:].unsqueeze(1).to_broadcast([P, P, PACK]),
+            op=ALU.mult,
+        )
         quantise(0)
         nc.vector.quantize_mx(
             out=h_codes[:].bitcast(FP8X4),
@@ -207,7 +234,6 @@ def tile_rawkvinjector_pa_s_kernel(
             in_=h_grouped[:].rearrange("p t j -> p (t j)"),
         )
         multiply(0)
-
         quantise(1)
         multiply(1)
         regroup(nc.vector.tensor_copy, 2, vector_cols)
@@ -218,35 +244,6 @@ def tile_rawkvinjector_pa_s_kernel(
         multiply(2)
         quantise(3)
         multiply(3)
-
-        nw_bc = psum.tile([P, 2, HD], F32)
-        nc.tensor.matmul(
-            out=nw_bc[:].rearrange("p g d -> p (g d)"),
-            lhsT=ones[:],
-            rhs=rows[:, D : D + 2 * HD],
-            start=True,
-            stop=True,
-        )
-        nc.vector.tensor_tensor(
-            out=rope_cos[:],
-            in0=nw_bc[:],
-            in1=cos_sb[:].unsqueeze(1).to_broadcast([P, 2, HD]),
-            op=ALU.mult,
-        )
-        nc.vector.scalar_tensor_tensor(
-            out=rope_sin[:, :, 0:HALF],
-            in0=nw_bc[:, :, HALF:HD],
-            scalar=-1.0,
-            in1=sin_sb[:, 0:HALF].unsqueeze(1).to_broadcast([P, 2, HALF]),
-            op0=ALU.mult,
-            op1=ALU.mult,
-        )
-        nc.vector.tensor_tensor(
-            out=rope_sin[:, :, HALF:HD],
-            in0=nw_bc[:, :, 0:HALF],
-            in1=sin_sb[:, HALF:HD].unsqueeze(1).to_broadcast([P, 2, HALF]),
-            op=ALU.mult,
-        )
 
         normalise(0, 0, HEADS)
         rope(0, 0, HEADS)

@@ -28,42 +28,44 @@ def tile_rawkvinjector_pa_s_kernel(
     nc = tc.nc
     vector_cols = (0, CHUNK - SCALAR_COLS)
     scalar_cols = (CHUNK - SCALAR_COLS, CHUNK)
+    V_CHUNK = 0
     chunks = [
+        (Wv, 0, out_2, 0, None),
         (Wq, 0, out_0, 0, 0),
         (Wq, CHUNK, out_0, HEADS, 0),
         (Wk, 0, out_1, 0, 1),
-        (Wv, 0, out_2, 0, None),
     ]
+    every = range(4)
+    normed_chunks = range(1, 4)
     with (
         nc.allow_non_contiguous_dma(reason="outputs are stored head by head, 256 bytes a run"),
         tc.tile_pool(name="keep", bufs=1) as keep,
         tc.psum_pool(name="psum", bufs=1) as psum,
         tc.manual_schedule(),
     ):
-        raw = [keep.tile([P, PACK, CHUNK], BF16, name="raw%d" % c) for c in range(4)]
+        raw = [keep.tile([P, PACK, CHUNK], BF16, name="raw%d" % c) for c in every]
         grouped = [
-            keep.tile([P, CHUNK, PACK], BF16, name="grouped%d" % c, align_bytes=64) for c in range(4)
+            keep.tile([P, CHUNK, PACK], BF16, name="grouped%d" % c, align_bytes=64) for c in every
         ]
-        codes = [keep.tile([P, CHUNK], U32, name="codes%d" % c, align_bytes=64) for c in range(4)]
-        scales = [keep.tile([P, CHUNK], U8, name="scales%d" % c, align_bytes=64) for c in range(4)]
-        prod = [psum.tile([P, HEADS, HD], F32, name="prod%d" % c) for c in range(4)]
-        squares = [keep.tile([P, HEADS, HD], F32, name="squares%d" % c) for c in range(3)]
-        ssq = [keep.tile([P, HEADS], F32, name="ssq%d" % c) for c in range(3)]
-        rstd = [keep.tile([P, HEADS], F32, name="rstd%d" % c) for c in range(3)]
-        normed = [keep.tile([P, HEADS, HD], F32, name="normed%d" % c) for c in range(3)]
-        turned = [keep.tile([P, HEADS, HD], F32, name="turned%d" % c) for c in range(3)]
-        result = [keep.tile([P, HEADS, HD], F32, name="result%d" % c) for c in range(4)]
+        codes = [keep.tile([P, CHUNK], U32, name="codes%d" % c, align_bytes=64) for c in every]
+        scales = [keep.tile([P, CHUNK], U8, name="scales%d" % c, align_bytes=64) for c in every]
+        prod = [psum.tile([P, HEADS, HD], F32, name="prod%d" % c) for c in every]
+        result = [keep.tile([P, HEADS, HD], F32, name="result%d" % c) for c in every]
+        squares = {c: keep.tile([P, HEADS, HD], F32, name="squares%d" % c) for c in normed_chunks}
+        ssq = {c: keep.tile([P, HEADS], F32, name="ssq%d" % c) for c in normed_chunks}
+        rstd = {c: keep.tile([P, HEADS], F32, name="rstd%d" % c) for c in normed_chunks}
+        normed = {c: keep.tile([P, HEADS, HD], F32, name="normed%d" % c) for c in normed_chunks}
+        turned = {c: keep.tile([P, HEADS, HD], F32, name="turned%d" % c) for c in normed_chunks}
         h_codes = keep.tile([P, P], U32, align_bytes=64)
         h_scales = keep.tile([P, P], U8, align_bytes=64)
         rope_cos = keep.tile([P, 2, HD], F32)
         rope_sin = keep.tile([P, 2, HD], F32)
 
-        def load(c, cols):
+        def load(c):
             w, col0 = chunks[c][0], chunks[c][1]
-            lo, hi = cols
             nc.sync.dma_start(
-                out=raw[c][:, :, lo:hi],
-                in_=w.rearrange("(p j) n -> p j n", j=PACK)[:, :, col0 + lo : col0 + hi],
+                out=raw[c][:],
+                in_=w.rearrange("(p j) n -> p j n", j=PACK)[:, :, col0 : col0 + CHUNK],
             )
 
         def regroup(copy, c, cols):
@@ -73,14 +75,16 @@ def tile_rawkvinjector_pa_s_kernel(
                 in_=raw[c][:, :, lo:hi].rearrange("p j (n i) -> p n j i", i=4),
             )
 
-        def quantise(c):
+        def regroup_both(c):
+            regroup(nc.vector.tensor_copy, c, vector_cols)
+            regroup(nc.scalar.copy, c, scalar_cols)
+
+        def quantise_and_multiply(c):
             nc.vector.quantize_mx(
                 out=codes[c][:].bitcast(FP8X4),
                 scales=scales[c][:],
                 in_=grouped[c][:].rearrange("p n j -> p (n j)"),
             )
-
-        def multiply(c):
             nc.tensor.matmul_mx(
                 out=prod[c][:].rearrange("p h d -> p (h d)"),
                 lhsT=h_codes[:].bitcast(FP8X4),
@@ -91,7 +95,10 @@ def tile_rawkvinjector_pa_s_kernel(
                 stop=True,
             )
 
-        def normalise(c, h0, h1):
+        def copy_v_head(h):
+            nc.scalar.copy(out=result[V_CHUNK][:, h, :], in_=prod[V_CHUNK][:, h, :])
+
+        def normalise(c, h0, h1, v_head):
             for h in range(h0, h1):
                 nc.scalar.activation(
                     out=squares[c][:, h, :],
@@ -99,6 +106,7 @@ def tile_rawkvinjector_pa_s_kernel(
                     func=ACT.Square,
                     accum_out=ssq[c][:, h : h + 1],
                 )
+            copy_v_head(v_head)
             nc.scalar.activation(
                 out=rstd[c][:, h0:h1],
                 in_=ssq[c][:, h0:h1],
@@ -106,6 +114,7 @@ def tile_rawkvinjector_pa_s_kernel(
                 scale=1.0 / HD,
                 bias=EPS,
             )
+            copy_v_head(v_head + 1)
             for h in range(h0, h1):
                 nc.scalar.activation(
                     out=normed[c][:, h, :],
@@ -153,10 +162,6 @@ def tile_rawkvinjector_pa_s_kernel(
         nc.sync.dma_start(out=x[:], in_=hidden_states.rearrange("b t d -> (b t) d"))
         ln_w = keep.tile([P, PACK], BF16)
         nc.sync.dma_start(out=ln_w[:], in_=ln1_w.rearrange("(p j) -> p j", j=PACK))
-        load(0, vector_cols)
-        load(0, scalar_cols)
-        for c in range(1, 4):
-            load(c, (0, CHUNK))
         cos_sb = keep.tile([P, HD], BF16)
         nc.sync.dma_start(out=cos_sb[:], in_=cos)
         sin_sb = keep.tile([P, HD], BF16)
@@ -164,6 +169,8 @@ def tile_rawkvinjector_pa_s_kernel(
         norm_w = keep.tile([P, 2, HD], BF16)
         nc.sync.dma_start(out=norm_w[:, 0, :], in_=q_norm_w.partition_broadcast(P))
         nc.sync.dma_start(out=norm_w[:, 1, :], in_=k_norm_w.partition_broadcast(P))
+        for c in every:
+            load(c)
 
         ident = keep.tile([P, P], F32)
         make_identity(nc, ident[:])
@@ -171,31 +178,25 @@ def tile_rawkvinjector_pa_s_kernel(
         nc.vector.memset(warm[:], 1.0)
         nc.scalar.activation(out=warm[:], in_=warm[:], func=ACT.Abs_reciprocal_sqrt)
 
-        nc.gpsimd.tensor_tensor(
+        nc.vector.tensor_tensor(
             out=rope_cos[:],
             in0=norm_w[:],
             in1=cos_sb[:].unsqueeze(1).to_broadcast([P, 2, HD]),
             op=ALU.mult,
         )
-        nc.gpsimd.tensor_tensor(
+        nc.vector.scalar_tensor_tensor(
+            out=rope_sin[:, :, 0:HALF],
+            in0=norm_w[:, :, HALF:HD],
+            scalar=-1.0,
+            in1=sin_sb[:, 0:HALF].unsqueeze(1).to_broadcast([P, 2, HALF]),
+            op0=ALU.mult,
+            op1=ALU.mult,
+        )
+        nc.vector.tensor_tensor(
             out=rope_sin[:, :, HALF:HD],
             in0=norm_w[:, :, 0:HALF],
             in1=sin_sb[:, HALF:HD].unsqueeze(1).to_broadcast([P, 2, HALF]),
             op=ALU.mult,
-        )
-        nc.gpsimd.tensor_tensor(
-            out=rope_sin[:, :, 0:HALF],
-            in0=norm_w[:, :, HALF:HD],
-            in1=sin_sb[:, 0:HALF].unsqueeze(1).to_broadcast([P, 2, HALF]),
-            op=ALU.mult,
-        )
-        nc.gpsimd.tensor_scalar(
-            out=rope_sin[:, :, 0:HALF],
-            in0=rope_sin[:, :, 0:HALF],
-            scalar1=-1.0,
-            scalar2=0.0,
-            op0=ALU.mult,
-            op1=ALU.add,
         )
 
         x_sq = keep.tile([P, D], BF16)
@@ -205,8 +206,6 @@ def tile_rawkvinjector_pa_s_kernel(
         nc.scalar.activation(
             out=x_rstd[:], in_=x_ssq[:], func=ACT.Abs_reciprocal_sqrt, scale=1.0 / D, bias=EPS
         )
-        regroup(nc.vector.tensor_copy, 0, vector_cols)
-        regroup(nc.scalar.copy, 0, scalar_cols)
         x_normed = keep.tile([P, PACK, P], F32)
         nc.vector.tensor_scalar(
             out=x_normed[:],
@@ -218,8 +217,7 @@ def tile_rawkvinjector_pa_s_kernel(
         x_turned = psum.tile([P, PACK, P], F32)
         for j in range(PACK):
             nc.tensor.transpose(x_turned[:, j, :], x_normed[:, j, :], ident[:])
-        regroup(nc.vector.tensor_copy, 1, vector_cols)
-        regroup(nc.scalar.copy, 1, scalar_cols)
+        regroup_both(0)
         h_grouped = keep.tile([P, P, PACK], BF16, align_bytes=64)
         nc.vector.tensor_tensor(
             out=h_grouped[:],
@@ -227,35 +225,30 @@ def tile_rawkvinjector_pa_s_kernel(
             in1=ln_w[:].unsqueeze(1).to_broadcast([P, P, PACK]),
             op=ALU.mult,
         )
-        quantise(0)
+        regroup_both(1)
         nc.vector.quantize_mx(
             out=h_codes[:].bitcast(FP8X4),
             scales=h_scales[:],
             in_=h_grouped[:].rearrange("p t j -> p (t j)"),
         )
-        multiply(0)
-        quantise(1)
-        multiply(1)
-        regroup(nc.vector.tensor_copy, 2, vector_cols)
-        regroup(nc.scalar.copy, 2, scalar_cols)
-        regroup(nc.vector.tensor_copy, 3, vector_cols)
-        regroup(nc.scalar.copy, 3, scalar_cols)
-        quantise(2)
-        multiply(2)
-        quantise(3)
-        multiply(3)
+        quantise_and_multiply(0)
+        quantise_and_multiply(1)
+        regroup_both(2)
+        regroup_both(3)
+        quantise_and_multiply(2)
+        quantise_and_multiply(3)
 
-        normalise(0, 0, HEADS)
-        rope(0, 0, HEADS)
-        store(0, 0, HEADS)
-        normalise(1, 0, HEADS)
+        normalise(1, 0, HEADS, 0)
         rope(1, 0, HEADS)
         store(1, 0, HEADS)
-        normalise(2, 0, HEADS // 2)
-        rope(2, 0, HEADS // 2)
-        store(2, 0, HEADS // 2)
-        normalise(2, HEADS // 2, HEADS)
-        rope(2, HEADS // 2, HEADS)
-        store(2, HEADS // 2, HEADS)
-        nc.scalar.copy(out=result[3][:], in_=prod[3][:])
-        store(3, 0, HEADS)
+        normalise(2, 0, HEADS, 2)
+        store(V_CHUNK, 0, HEADS // 2)
+        rope(2, 0, HEADS)
+        store(2, 0, HEADS)
+        normalise(3, 0, HEADS // 2, 4)
+        rope(3, 0, HEADS // 2)
+        store(3, 0, HEADS // 2)
+        normalise(3, HEADS // 2, HEADS, 6)
+        store(V_CHUNK, HEADS // 2, HEADS)
+        rope(3, HEADS // 2, HEADS)
+        store(3, HEADS // 2, HEADS)

@@ -17,7 +17,7 @@ HALF = HD // 2
 CHUNK = 512
 HEADS = CHUNK // HD
 EPS = 1e-6
-SCALAR_COLS = 256
+SCALAR_COLS = 128
 
 FLOPS = 2 * P * D * 4 * CHUNK
 

@@ -95,10 +95,10 @@ def tile_rawkvinjector_pa_s_kernel(
                 stop=True,
             )
 
-        def copy_v_head(h):
-            nc.scalar.copy(out=result[V_CHUNK][:, h, :], in_=prod[V_CHUNK][:, h, :])
+        def copy_v(h0, h1):
+            nc.scalar.copy(out=result[V_CHUNK][:, h0:h1, :], in_=prod[V_CHUNK][:, h0:h1, :])
 
-        def normalise(c, h0, h1, v_head):
+        def sum_squares(c, h0, h1):
             for h in range(h0, h1):
                 nc.scalar.activation(
                     out=squares[c][:, h, :],
@@ -106,50 +106,54 @@ def tile_rawkvinjector_pa_s_kernel(
                     func=ACT.Square,
                     accum_out=ssq[c][:, h : h + 1],
                 )
-            copy_v_head(v_head)
+
+        def inverse_rms(c):
             nc.scalar.activation(
-                out=rstd[c][:, h0:h1],
-                in_=ssq[c][:, h0:h1],
+                out=rstd[c][:],
+                in_=ssq[c][:],
                 func=ACT.Abs_reciprocal_sqrt,
                 scale=1.0 / HD,
                 bias=EPS,
             )
-            copy_v_head(v_head + 1)
-            for h in range(h0, h1):
-                nc.scalar.activation(
-                    out=normed[c][:, h, :],
-                    in_=prod[c][:, h, :],
-                    func=ACT.Copy,
-                    scale=rstd[c][:, h : h + 1],
-                )
 
-        def rope(c, h0, h1):
+        def rope_products(c, h0, h1):
             norm = chunks[c][4]
             n = h1 - h0
             nc.vector.tensor_tensor(
                 out=turned[c][:, h0:h1, 0:HALF],
-                in0=normed[c][:, h0:h1, HALF:HD],
+                in0=prod[c][:, h0:h1, HALF:HD],
                 in1=rope_sin[:, norm, 0:HALF].unsqueeze(1).to_broadcast([P, n, HALF]),
                 op=ALU.mult,
             )
             nc.vector.tensor_tensor(
                 out=turned[c][:, h0:h1, HALF:HD],
-                in0=normed[c][:, h0:h1, 0:HALF],
+                in0=prod[c][:, h0:h1, 0:HALF],
                 in1=rope_sin[:, norm, HALF:HD].unsqueeze(1).to_broadcast([P, n, HALF]),
                 op=ALU.mult,
             )
             nc.vector.tensor_tensor(
-                out=result[c][:, h0:h1, :],
-                in0=normed[c][:, h0:h1, :],
+                out=normed[c][:, h0:h1, :],
+                in0=prod[c][:, h0:h1, :],
                 in1=rope_cos[:, norm, :].unsqueeze(1).to_broadcast([P, n, HD]),
                 op=ALU.mult,
             )
-            nc.vector.tensor_tensor(
-                out=result[c][:, h0:h1, :],
-                in0=result[c][:, h0:h1, :],
+
+        def rope_add(engine, c, h0, h1):
+            engine.tensor_tensor(
+                out=normed[c][:, h0:h1, :],
+                in0=normed[c][:, h0:h1, :],
                 in1=turned[c][:, h0:h1, :],
                 op=ALU.add,
             )
+
+        def scale_heads(c, h0, h1):
+            for h in range(h0, h1):
+                nc.scalar.activation(
+                    out=result[c][:, h, :],
+                    in_=normed[c][:, h, :],
+                    func=ACT.Copy,
+                    scale=rstd[c][:, h : h + 1],
+                )
 
         def store(c, h0, h1):
             out, head0 = chunks[c][2], chunks[c][3]
@@ -238,17 +242,31 @@ def tile_rawkvinjector_pa_s_kernel(
         quantise_and_multiply(2)
         quantise_and_multiply(3)
 
-        normalise(1, 0, HEADS, 0)
-        rope(1, 0, HEADS)
+        HH = HEADS // 2
+        copy_v(0, HH)
+        store(V_CHUNK, 0, HH)
+        sum_squares(1, 0, HEADS)
+        copy_v(HH, HEADS)
+        store(V_CHUNK, HH, HEADS)
+        inverse_rms(1)
+        sum_squares(2, 0, HEADS)
+        rope_products(1, 0, HEADS)
+        rope_add(nc.gpsimd, 1, 0, HEADS)
+        sum_squares(3, 0, HH)
+        inverse_rms(2)
+        sum_squares(3, HH, HEADS)
+        rope_products(2, 0, HEADS)
+        rope_add(nc.gpsimd, 2, 0, HEADS)
+        scale_heads(1, 0, HEADS)
         store(1, 0, HEADS)
-        normalise(2, 0, HEADS, 2)
-        store(V_CHUNK, 0, HEADS // 2)
-        rope(2, 0, HEADS)
+        inverse_rms(3)
+        rope_products(3, 0, HH)
+        rope_add(nc.gpsimd, 3, 0, HH)
+        rope_products(3, HH, HEADS)
+        rope_add(nc.vector, 3, HH, HEADS)
+        scale_heads(2, 0, HEADS)
         store(2, 0, HEADS)
-        normalise(3, 0, HEADS // 2, 4)
-        rope(3, 0, HEADS // 2)
-        store(3, 0, HEADS // 2)
-        normalise(3, HEADS // 2, HEADS, 6)
-        store(V_CHUNK, HEADS // 2, HEADS)
-        rope(3, HEADS // 2, HEADS)
-        store(3, HEADS // 2, HEADS)
+        scale_heads(3, 0, HH)
+        store(3, 0, HH)
+        scale_heads(3, HH, HEADS)
+        store(3, HH, HEADS)

@@ -17,7 +17,7 @@ HALF = HD // 2
 CHUNK = 512
 HEADS = CHUNK // HD
 EPS = 1e-6
-SCALAR_COLS = 128
+SCALAR_COLS = 192
 
 FLOPS = 2 * P * D * 4 * CHUNK
 
@@ -116,7 +116,7 @@ def tile_rawkvinjector_pa_s_kernel(
                 bias=EPS,
             )
 
-        def rope_products(c, h0, h1):
+        def rope_turned(c, h0, h1):
             norm = chunks[c][4]
             n = h1 - h0
             nc.vector.tensor_tensor(
@@ -131,6 +131,10 @@ def tile_rawkvinjector_pa_s_kernel(
                 in1=rope_sin[:, norm, HALF:HD].unsqueeze(1).to_broadcast([P, n, HALF]),
                 op=ALU.mult,
             )
+
+        def rope_straight(c, h0, h1):
+            norm = chunks[c][4]
+            n = h1 - h0
             nc.vector.tensor_tensor(
                 out=normed[c][:, h0:h1, :],
                 in0=prod[c][:, h0:h1, :],
@@ -250,22 +254,33 @@ def tile_rawkvinjector_pa_s_kernel(
         store(V_CHUNK, HH, HEADS)
         inverse_rms(1)
         sum_squares(2, 0, HEADS)
-        rope_products(1, 0, HEADS)
-        rope_add(nc.gpsimd, 1, 0, HEADS)
+        rope_turned(1, 0, HEADS)
+        rope_straight(1, 0, HH)
+        rope_add(nc.gpsimd, 1, 0, HH)
+        rope_straight(1, HH, HEADS)
+        rope_add(nc.gpsimd, 1, HH, HEADS)
         sum_squares(3, 0, HH)
         inverse_rms(2)
         sum_squares(3, HH, HEADS)
-        rope_products(2, 0, HEADS)
-        rope_add(nc.gpsimd, 2, 0, HEADS)
-        scale_heads(1, 0, HEADS)
-        store(1, 0, HEADS)
+        scale_heads(1, 0, HH)
+        store(1, 0, HH)
         inverse_rms(3)
-        rope_products(3, 0, HH)
+        rope_turned(2, 0, HEADS)
+        rope_straight(2, 0, HH)
+        rope_add(nc.gpsimd, 2, 0, HH)
+        rope_straight(2, HH, HEADS)
+        rope_add(nc.gpsimd, 2, HH, HEADS)
+        scale_heads(1, HH, HEADS)
+        store(1, HH, HEADS)
+        rope_turned(3, 0, HEADS)
+        rope_straight(3, 0, HH)
         rope_add(nc.gpsimd, 3, 0, HH)
-        rope_products(3, HH, HEADS)
+        rope_straight(3, HH, HEADS)
         rope_add(nc.vector, 3, HH, HEADS)
-        scale_heads(2, 0, HEADS)
-        store(2, 0, HEADS)
+        scale_heads(2, 0, HH)
+        store(2, 0, HH)
+        scale_heads(2, HH, HEADS)
+        store(2, HH, HEADS)
         scale_heads(3, 0, HH)
         store(3, 0, HH)
         scale_heads(3, HH, HEADS)

@@ -274,8 +274,8 @@ def tile_rawkvinjector_pa_s_kernel(
         store(1, HH, HEADS)
         rope_turned(3, 0, HEADS)
         rope_straight(3, 0, HH)
-        rope_add(nc.gpsimd, 3, 0, HH)
         rope_straight(3, HH, HEADS)
+        rope_add(nc.vector, 3, 0, HH)
         rope_add(nc.vector, 3, HH, HEADS)
         scale_heads(2, 0, HH)
         store(2, 0, HH)

@@ -20,6 +20,9 @@ EPS = 1e-6
 SCALAR_COLS = 192
 
 FLOPS = 2 * P * D * 4 * CHUNK
+PLAIN_WARMERS = 4
+assert PLAIN_WARMERS * 2 * P * P * P <= FLOPS // 10
+MX_WARMERS = 4
 
 
 def tile_rawkvinjector_pa_s_kernel(
@@ -186,6 +189,10 @@ def tile_rawkvinjector_pa_s_kernel(
         nc.vector.memset(warm[:], 1.0)
         nc.scalar.activation(out=warm[:], in_=warm[:], func=ACT.Abs_reciprocal_sqrt)
 
+        spare = psum.tile([P, CHUNK], F32)
+        for w in range(PLAIN_WARMERS):
+            nc.tensor.matmul(out=spare[:, 0:P], lhsT=ident[:], rhs=ident[:], start=True, stop=True)
+
         nc.vector.tensor_tensor(
             out=rope_cos[:],
             in0=norm_w[:],
@@ -241,6 +248,16 @@ def tile_rawkvinjector_pa_s_kernel(
         )
         quantise_and_multiply(0)
         quantise_and_multiply(1)
+        for w in range(MX_WARMERS):
+            nc.tensor.matmul_mx(
+                out=spare[:],
+                lhsT=h_codes[:].bitcast(FP8X4),
+                lhsT_scale=h_scales[:],
+                rhs=codes[1][:].bitcast(FP8X4),
+                rhs_scale=scales[1][:],
+                start=True,
+                stop=True,
+            )
         regroup_both(2)
         regroup_both(3)
         quantise_and_multiply(2)

@@ -17,12 +17,9 @@ HALF = HD // 2
 CHUNK = 512
 HEADS = CHUNK // HD
 EPS = 1e-6
-SCALAR_COLS = 192
+SCALAR_COLS = 224
 
 FLOPS = 2 * P * D * 4 * CHUNK
-PLAIN_WARMERS = 4
-assert PLAIN_WARMERS * 2 * P * P * P <= FLOPS // 10
-MX_WARMERS = 4
 
 
 def tile_rawkvinjector_pa_s_kernel(
@@ -34,9 +31,9 @@ def tile_rawkvinjector_pa_s_kernel(
     V_CHUNK = 0
     chunks = [
         (Wv, 0, out_2, 0, None),
+        (Wk, 0, out_1, 0, 1),
         (Wq, 0, out_0, 0, 0),
         (Wq, CHUNK, out_0, HEADS, 0),
-        (Wk, 0, out_1, 0, 1),
     ]
     every = range(4)
     normed_chunks = range(1, 4)
@@ -53,6 +50,7 @@ def tile_rawkvinjector_pa_s_kernel(
         codes = [keep.tile([P, CHUNK], U32, name="codes%d" % c, align_bytes=64) for c in every]
         scales = [keep.tile([P, CHUNK], U8, name="scales%d" % c, align_bytes=64) for c in every]
         prod = [psum.tile([P, HEADS, HD], F32, name="prod%d" % c) for c in every]
+        prod_sq = {c: psum.tile([P, HEADS, HD], F32, name="prod_sq%d" % c) for c in normed_chunks}
         result = [keep.tile([P, HEADS, HD], F32, name="result%d" % c) for c in every]
         squares = {c: keep.tile([P, HEADS, HD], F32, name="squares%d" % c) for c in normed_chunks}
         ssq = {c: keep.tile([P, HEADS], F32, name="ssq%d" % c) for c in normed_chunks}
@@ -78,25 +76,22 @@ def tile_rawkvinjector_pa_s_kernel(
                 in_=raw[c][:, :, lo:hi].rearrange("p j (n i) -> p n j i", i=4),
             )
 
-        def regroup_both(c):
-            regroup(nc.vector.tensor_copy, c, vector_cols)
-            regroup(nc.scalar.copy, c, scalar_cols)
-
         def quantise_and_multiply(c):
             nc.vector.quantize_mx(
                 out=codes[c][:].bitcast(FP8X4),
                 scales=scales[c][:],
                 in_=grouped[c][:].rearrange("p n j -> p (n j)"),
             )
-            nc.tensor.matmul_mx(
-                out=prod[c][:].rearrange("p h d -> p (h d)"),
-                lhsT=h_codes[:].bitcast(FP8X4),
-                lhsT_scale=h_scales[:],
-                rhs=codes[c][:].bitcast(FP8X4),
-                rhs_scale=scales[c][:],
-                start=True,
-                stop=True,
-            )
+            for bank in (prod[c],) if c == V_CHUNK else (prod_sq[c], prod[c]):
+                nc.tensor.matmul_mx(
+                    out=bank[:].rearrange("p h d -> p (h d)"),
+                    lhsT=h_codes[:].bitcast(FP8X4),
+                    lhsT_scale=h_scales[:],
+                    rhs=codes[c][:].bitcast(FP8X4),
+                    rhs_scale=scales[c][:],
+                    start=True,
+                    stop=True,
+                )
 
         def copy_v(h0, h1):
             nc.scalar.copy(out=result[V_CHUNK][:, h0:h1, :], in_=prod[V_CHUNK][:, h0:h1, :])
@@ -105,7 +100,7 @@ def tile_rawkvinjector_pa_s_kernel(
             for h in range(h0, h1):
                 nc.scalar.activation(
                     out=squares[c][:, h, :],
-                    in_=prod[c][:, h, :],
+                    in_=prod_sq[c][:, h, :],
                     func=ACT.Square,
                     accum_out=ssq[c][:, h : h + 1],
                 )
@@ -171,8 +166,8 @@ def tile_rawkvinjector_pa_s_kernel(
 
         x = keep.tile([P, D], BF16)
         nc.sync.dma_start(out=x[:], in_=hidden_states.rearrange("b t d -> (b t) d"))
-        ln_w = keep.tile([P, PACK], BF16)
-        nc.sync.dma_start(out=ln_w[:], in_=ln1_w.rearrange("(p j) -> p j", j=PACK))
+        ln_w = keep.tile([P, D], BF16)
+        nc.sync.dma_start(out=ln_w[:], in_=ln1_w.partition_broadcast(P))
         cos_sb = keep.tile([P, HD], BF16)
         nc.sync.dma_start(out=cos_sb[:], in_=cos)
         sin_sb = keep.tile([P, HD], BF16)
@@ -188,10 +183,6 @@ def tile_rawkvinjector_pa_s_kernel(
         warm = keep.tile([P, 1], F32)
         nc.vector.memset(warm[:], 1.0)
         nc.scalar.activation(out=warm[:], in_=warm[:], func=ACT.Abs_reciprocal_sqrt)
-
-        spare = psum.tile([P, CHUNK], F32)
-        for w in range(PLAIN_WARMERS):
-            nc.tensor.matmul(out=spare[:, 0:P], lhsT=ident[:], rhs=ident[:], start=True, stop=True)
 
         nc.vector.tensor_tensor(
             out=rope_cos[:],
@@ -221,84 +212,67 @@ def tile_rawkvinjector_pa_s_kernel(
         nc.scalar.activation(
             out=x_rstd[:], in_=x_ssq[:], func=ACT.Abs_reciprocal_sqrt, scale=1.0 / D, bias=EPS
         )
-        x_normed = keep.tile([P, PACK, P], F32)
-        nc.vector.tensor_scalar(
-            out=x_normed[:],
-            in0=x[:].rearrange("t (p j) -> t j p", j=PACK),
-            scalar1=x_rstd[:],
-            scalar2=None,
-            op0=ALU.mult,
+        h = keep.tile([P, D], BF16)
+        nc.vector.scalar_tensor_tensor(
+            out=h[:], in0=x[:], scalar=x_rstd[:], in1=ln_w[:], op0=ALU.mult, op1=ALU.mult
         )
-        x_turned = psum.tile([P, PACK, P], F32)
-        for j in range(PACK):
-            nc.tensor.transpose(x_turned[:, j, :], x_normed[:, j, :], ident[:])
-        regroup_both(0)
+        h_words = h[:].bitcast(F32)
+        h_turned = psum.tile([P, 2, P], F32)
+        for u in range(2):
+            nc.tensor.transpose(h_turned[:, u, :], h_words[:, u::2], ident[:])
+        regroup(nc.vector.tensor_copy, 0, vector_cols)
         h_grouped = keep.tile([P, P, PACK], BF16, align_bytes=64)
-        nc.vector.tensor_tensor(
-            out=h_grouped[:],
-            in0=x_turned[:].rearrange("p j t -> p t j"),
-            in1=ln_w[:].unsqueeze(1).to_broadcast([P, P, PACK]),
-            op=ALU.mult,
+        nc.vector.tensor_copy(
+            out=h_grouped[:].bitcast(F32), in_=h_turned[:].rearrange("p u t -> p t u")
         )
-        regroup_both(1)
+        regroup(nc.vector.tensor_copy, 1, vector_cols)
+        for c in every:
+            regroup(nc.scalar.copy, c, scalar_cols)
         nc.vector.quantize_mx(
             out=h_codes[:].bitcast(FP8X4),
             scales=h_scales[:],
             in_=h_grouped[:].rearrange("p t j -> p (t j)"),
         )
         quantise_and_multiply(0)
+        regroup(nc.vector.tensor_copy, 2, vector_cols)
         quantise_and_multiply(1)
-        for w in range(MX_WARMERS):
-            nc.tensor.matmul_mx(
-                out=spare[:],
-                lhsT=h_codes[:].bitcast(FP8X4),
-                lhsT_scale=h_scales[:],
-                rhs=codes[1][:].bitcast(FP8X4),
-                rhs_scale=scales[1][:],
-                start=True,
-                stop=True,
-            )
-        regroup_both(2)
-        regroup_both(3)
+        regroup(nc.vector.tensor_copy, 3, vector_cols)
         quantise_and_multiply(2)
         quantise_and_multiply(3)
 
         HH = HEADS // 2
-        copy_v(0, HH)
-        store(V_CHUNK, 0, HH)
         sum_squares(1, 0, HEADS)
-        copy_v(HH, HEADS)
-        store(V_CHUNK, HH, HEADS)
+        copy_v(0, HEADS)
+        store(V_CHUNK, 0, HEADS)
         inverse_rms(1)
         sum_squares(2, 0, HEADS)
-        rope_turned(1, 0, HEADS)
-        rope_straight(1, 0, HH)
-        rope_add(nc.gpsimd, 1, 0, HH)
-        rope_straight(1, HH, HEADS)
-        rope_add(nc.gpsimd, 1, HH, HEADS)
-        sum_squares(3, 0, HH)
-        inverse_rms(2)
-        sum_squares(3, HH, HEADS)
+        for c in (1, 2):
+            for h0 in (0, HH):
+                rope_turned(c, h0, h0 + HH)
+                rope_straight(c, h0, h0 + HH)
+                rope_add(nc.gpsimd, c, h0, h0 + HH)
         scale_heads(1, 0, HH)
         store(1, 0, HH)
-        inverse_rms(3)
-        rope_turned(2, 0, HEADS)
-        rope_straight(2, 0, HH)
-        rope_add(nc.gpsimd, 2, 0, HH)
-        rope_straight(2, HH, HEADS)
-        rope_add(nc.gpsimd, 2, HH, HEADS)
+        sum_squares(3, 0, HH)
         scale_heads(1, HH, HEADS)
         store(1, HH, HEADS)
-        rope_turned(3, 0, HEADS)
-        rope_straight(3, 0, HH)
-        rope_straight(3, HH, HEADS)
-        rope_add(nc.vector, 3, 0, HH)
-        rope_add(nc.vector, 3, HH, HEADS)
+        sum_squares(3, HH, HEADS)
+        inverse_rms(2)
+        inverse_rms(3)
         scale_heads(2, 0, HH)
         store(2, 0, HH)
         scale_heads(2, HH, HEADS)
         store(2, HH, HEADS)
-        scale_heads(3, 0, HH)
-        store(3, 0, HH)
-        scale_heads(3, HH, HEADS)
-        store(3, HH, HEADS)
+        rope_turned(3, 0, HEADS)
+        rope_straight(3, 0, HH)
+        rope_straight(3, HH, HEADS)
+        for h0 in (0, HH):
+            rope_add(nc.vector, 3, h0, h0 + HH)
+        for h0 in (0, HH):
+            nc.vector.tensor_tensor(
+                out=result[3][:, h0 : h0 + HH, :],
+                in0=normed[3][:, h0 : h0 + HH, :],
+                in1=rstd[3][:, h0 : h0 + HH].unsqueeze(2).to_broadcast([P, HH, HD]),
+                op=ALU.mult,
+            )
+            store(3, h0, h0 + HH)

@@ -49,7 +49,8 @@ def tile_rawkvinjector_pa_s_kernel(
         ]
         codes = [keep.tile([P, CHUNK], U32, name="codes%d" % c, align_bytes=64) for c in every]
         scales = [keep.tile([P, CHUNK], U8, name="scales%d" % c, align_bytes=64) for c in every]
-        prod = [psum.tile([P, HEADS, HD], F32, name="prod%d" % c) for c in every]
+        ln_rows = psum.tile([P, PACK, P], F32, name="ln_rows", tag="prod3")
+        prod = [psum.tile([P, HEADS, HD], F32, name="prod%d" % c, tag="prod%d" % c) for c in range(3)]
         prod_sq = {c: psum.tile([P, HEADS, HD], F32, name="prod_sq%d" % c) for c in normed_chunks}
         result = [keep.tile([P, HEADS, HD], F32, name="result%d" % c) for c in every]
         squares = {c: keep.tile([P, HEADS, HD], F32, name="squares%d" % c) for c in normed_chunks}
@@ -166,8 +167,8 @@ def tile_rawkvinjector_pa_s_kernel(
 
         x = keep.tile([P, D], BF16)
         nc.sync.dma_start(out=x[:], in_=hidden_states.rearrange("b t d -> (b t) d"))
-        ln_w = keep.tile([P, D], BF16)
-        nc.sync.dma_start(out=ln_w[:], in_=ln1_w.partition_broadcast(P))
+        ln_w = keep.tile([P, PACK], BF16)
+        nc.sync.dma_start(out=ln_w[:], in_=ln1_w.rearrange("(p j) -> p j", j=PACK))
         cos_sb = keep.tile([P, HD], BF16)
         nc.sync.dma_start(out=cos_sb[:], in_=cos)
         sin_sb = keep.tile([P, HD], BF16)
@@ -180,6 +181,8 @@ def tile_rawkvinjector_pa_s_kernel(
 
         ident = keep.tile([P, P], F32)
         make_identity(nc, ident[:])
+        ident_bf = keep.tile([P, P], BF16)
+        nc.vector.tensor_copy(out=ident_bf[:], in_=ident[:])
         warm = keep.tile([P, 1], F32)
         nc.vector.memset(warm[:], 1.0)
         nc.scalar.activation(out=warm[:], in_=warm[:], func=ACT.Abs_reciprocal_sqrt)
@@ -212,10 +215,24 @@ def tile_rawkvinjector_pa_s_kernel(
         nc.scalar.activation(
             out=x_rstd[:], in_=x_ssq[:], func=ACT.Abs_reciprocal_sqrt, scale=1.0 / D, bias=EPS
         )
+        for j in range(PACK):
+            nc.tensor.matmul(
+                out=ln_rows[:, j, :],
+                lhsT=ln_w[:, j : j + 1].to_broadcast([P, P]),
+                rhs=ident_bf[:],
+                start=True,
+                stop=True,
+            )
         h = keep.tile([P, D], BF16)
         nc.vector.scalar_tensor_tensor(
-            out=h[:], in0=x[:], scalar=x_rstd[:], in1=ln_w[:], op0=ALU.mult, op1=ALU.mult
+            out=h[:].rearrange("t (p j) -> t p j", j=PACK),
+            in0=x[:].rearrange("t (p j) -> t p j", j=PACK),
+            scalar=x_rstd[:],
+            in1=ln_rows[:].rearrange("t j p -> t p j"),
+            op0=ALU.mult,
+            op1=ALU.mult,
         )
+        prod.append(psum.tile([P, HEADS, HD], F32, name="prod3", tag="prod3"))
         h_words = h[:].bitcast(F32)
         h_turned = psum.tile([P, 2, P], F32)
         for u in range(2):

@@ -50,7 +50,7 @@ def tile_rawkvinjector_pa_s_kernel(
         codes = [keep.tile([P, CHUNK], U32, name="codes%d" % c, align_bytes=64) for c in every]
         scales = [keep.tile([P, CHUNK], U8, name="scales%d" % c, align_bytes=64) for c in every]
         ln_rows = psum.tile([P, PACK, P], F32, name="ln_rows", tag="prod3")
-        prod = [psum.tile([P, HEADS, HD], F32, name="prod%d" % c, tag="prod%d" % c) for c in range(3)]
+        prod = [psum.tile([P, HEADS, HD], F32, name="prod%d" % c, tag="prod%d" % c) for c in range(2)]
         prod_sq = {c: psum.tile([P, HEADS, HD], F32, name="prod_sq%d" % c) for c in normed_chunks}
         result = [keep.tile([P, HEADS, HD], F32, name="result%d" % c) for c in every]
         squares = {c: keep.tile([P, HEADS, HD], F32, name="squares%d" % c) for c in normed_chunks}
@@ -173,9 +173,12 @@ def tile_rawkvinjector_pa_s_kernel(
         nc.sync.dma_start(out=cos_sb[:], in_=cos)
         sin_sb = keep.tile([P, HD], BF16)
         nc.sync.dma_start(out=sin_sb[:], in_=sin)
-        norm_w = keep.tile([P, 2, HD], BF16)
-        nc.sync.dma_start(out=norm_w[:, 0, :], in_=q_norm_w.partition_broadcast(P))
-        nc.sync.dma_start(out=norm_w[:, 1, :], in_=k_norm_w.partition_broadcast(P))
+        norm_row = keep.tile([P, 2, HD], BF16)
+        nc.vector.memset(norm_row[:], 0.0)
+        nc.sync.dma_start(out=norm_row[0:1, 0, :], in_=q_norm_w.unsqueeze(0))
+        nc.sync.dma_start(out=norm_row[0:1, 1, :], in_=k_norm_w.unsqueeze(0))
+        ones = keep.tile([P, P], BF16)
+        nc.vector.memset(ones[:], 1.0)
         for c in every:
             load(c)
 
@@ -186,6 +189,15 @@ def tile_rawkvinjector_pa_s_kernel(
         warm = keep.tile([P, 1], F32)
         nc.vector.memset(warm[:], 1.0)
         nc.scalar.activation(out=warm[:], in_=warm[:], func=ACT.Abs_reciprocal_sqrt)
+
+        norm_w = psum.tile([P, 2, HD], F32, name="norm_w", tag="prod2")
+        nc.tensor.matmul(
+            out=norm_w[:].rearrange("p i d -> p (i d)"),
+            lhsT=ones[:],
+            rhs=norm_row[:].rearrange("p i d -> p (i d)"),
+            start=True,
+            stop=True,
+        )
 
         nc.vector.tensor_tensor(
             out=rope_cos[:],
@@ -232,7 +244,8 @@ def tile_rawkvinjector_pa_s_kernel(
             op0=ALU.mult,
             op1=ALU.mult,
         )
-        prod.append(psum.tile([P, HEADS, HD], F32, name="prod3", tag="prod3"))
+        for c in (2, 3):
+            prod.append(psum.tile([P, HEADS, HD], F32, name="prod%d" % c, tag="prod%d" % c))
         h_words = h[:].bitcast(F32)
         h_turned = psum.tile([P, 2, P], F32)
         for u in range(2):

@@ -17,7 +17,7 @@ HALF = HD // 2
 CHUNK = 512
 HEADS = CHUNK // HD
 EPS = 1e-6
-SCALAR_COLS = 224
+SCALAR_COLS = 256
 
 FLOPS = 2 * P * D * 4 * CHUNK
 
@@ -60,8 +60,9 @@ def tile_rawkvinjector_pa_s_kernel(
         turned = {c: keep.tile([P, HEADS, HD], F32, name="turned%d" % c) for c in normed_chunks}
         h_codes = keep.tile([P, P], U32, align_bytes=64)
         h_scales = keep.tile([P, P], U8, align_bytes=64)
-        rope_cos = keep.tile([P, 2, HD], F32)
-        rope_sin = keep.tile([P, 2, HD], F32)
+        tables = keep.tile([P, 2, 2, HD], F32)
+        rope_cos = tables[:, 0, :, :]
+        rope_sin = tables[:, 1, :, :]
 
         def load(c):
             w, col0 = chunks[c][0], chunks[c][1]
@@ -169,18 +170,20 @@ def tile_rawkvinjector_pa_s_kernel(
         nc.sync.dma_start(out=x[:], in_=hidden_states.rearrange("b t d -> (b t) d"))
         ln_w = keep.tile([P, PACK], BF16)
         nc.sync.dma_start(out=ln_w[:], in_=ln1_w.rearrange("(p j) -> p j", j=PACK))
-        cos_sb = keep.tile([P, HD], BF16)
-        nc.sync.dma_start(out=cos_sb[:], in_=cos)
-        sin_sb = keep.tile([P, HD], BF16)
-        nc.sync.dma_start(out=sin_sb[:], in_=sin)
+        load(0)
+        angles = keep.tile([P, 2, HD], BF16)
+        nc.sync.dma_start(out=angles[:, 0, :], in_=cos)
+        nc.sync.dma_start(out=angles[:, 1, :], in_=sin)
         norm_row = keep.tile([P, 2, HD], BF16)
         nc.vector.memset(norm_row[:], 0.0)
         nc.sync.dma_start(out=norm_row[0:1, 0, :], in_=q_norm_w.unsqueeze(0))
         nc.sync.dma_start(out=norm_row[0:1, 1, :], in_=k_norm_w.unsqueeze(0))
+        for c in range(1, 4):
+            load(c)
         ones = keep.tile([P, P], BF16)
         nc.vector.memset(ones[:], 1.0)
-        for c in every:
-            load(c)
+        minus_ones = keep.tile([P, P], BF16)
+        nc.vector.memset(minus_ones[:], -1.0)
 
         ident = keep.tile([P, P], F32)
         make_identity(nc, ident[:])
@@ -189,36 +192,6 @@ def tile_rawkvinjector_pa_s_kernel(
         warm = keep.tile([P, 1], F32)
         nc.vector.memset(warm[:], 1.0)
         nc.scalar.activation(out=warm[:], in_=warm[:], func=ACT.Abs_reciprocal_sqrt)
-
-        norm_w = psum.tile([P, 2, HD], F32, name="norm_w", tag="prod2")
-        nc.tensor.matmul(
-            out=norm_w[:].rearrange("p i d -> p (i d)"),
-            lhsT=ones[:],
-            rhs=norm_row[:].rearrange("p i d -> p (i d)"),
-            start=True,
-            stop=True,
-        )
-
-        nc.vector.tensor_tensor(
-            out=rope_cos[:],
-            in0=norm_w[:],
-            in1=cos_sb[:].unsqueeze(1).to_broadcast([P, 2, HD]),
-            op=ALU.mult,
-        )
-        nc.vector.scalar_tensor_tensor(
-            out=rope_sin[:, :, 0:HALF],
-            in0=norm_w[:, :, HALF:HD],
-            scalar=-1.0,
-            in1=sin_sb[:, 0:HALF].unsqueeze(1).to_broadcast([P, 2, HALF]),
-            op0=ALU.mult,
-            op1=ALU.mult,
-        )
-        nc.vector.tensor_tensor(
-            out=rope_sin[:, :, HALF:HD],
-            in0=norm_w[:, :, 0:HALF],
-            in1=sin_sb[:, HALF:HD].unsqueeze(1).to_broadcast([P, 2, HALF]),
-            op=ALU.mult,
-        )
 
         x_sq = keep.tile([P, D], BF16)
         x_ssq = keep.tile([P, 1], F32)
@@ -244,17 +217,36 @@ def tile_rawkvinjector_pa_s_kernel(
             op0=ALU.mult,
             op1=ALU.mult,
         )
-        for c in (2, 3):
-            prod.append(psum.tile([P, HEADS, HD], F32, name="prod%d" % c, tag="prod%d" % c))
+        norm_w = psum.tile([P, 2, 2, HD], F32, name="norm_w", tag="prod2")
+        for turn, out_d, sign, in_d in (
+            (0, slice(0, HD), ones, slice(0, HD)),
+            (1, slice(0, HALF), minus_ones, slice(HALF, HD)),
+            (1, slice(HALF, HD), ones, slice(0, HALF)),
+        ):
+            nc.tensor.matmul(
+                out=norm_w[:, turn, :, out_d],
+                lhsT=sign[:],
+                rhs=norm_row[:, :, in_d],
+                start=True,
+                stop=True,
+            )
         h_words = h[:].bitcast(F32)
         h_turned = psum.tile([P, 2, P], F32)
         for u in range(2):
             nc.tensor.transpose(h_turned[:, u, :], h_words[:, u::2], ident[:])
         regroup(nc.vector.tensor_copy, 0, vector_cols)
+        nc.vector.tensor_tensor(
+            out=tables[:],
+            in0=norm_w[:],
+            in1=angles[:].unsqueeze(2).to_broadcast([P, 2, 2, HD]),
+            op=ALU.mult,
+        )
         h_grouped = keep.tile([P, P, PACK], BF16, align_bytes=64)
         nc.vector.tensor_copy(
             out=h_grouped[:].bitcast(F32), in_=h_turned[:].rearrange("p u t -> p t u")
         )
+        for c in (2, 3):
+            prod.append(psum.tile([P, HEADS, HD], F32, name="prod%d" % c, tag="prod%d" % c))
         regroup(nc.vector.tensor_copy, 1, vector_cols)
         for c in every:
             regroup(nc.scalar.copy, c, scalar_cols)

@@ -268,11 +268,16 @@ def tile_rawkvinjector_pa_s_kernel(
         store(V_CHUNK, 0, HEADS)
         inverse_rms(1)
         sum_squares(2, 0, HEADS)
-        for c in (1, 2):
-            for h0 in (0, HH):
-                rope_turned(c, h0, h0 + HH)
-                rope_straight(c, h0, h0 + HH)
-                rope_add(nc.gpsimd, c, h0, h0 + HH)
+        for h0 in (0, HH):
+            rope_turned(1, h0, h0 + HH)
+            rope_straight(1, h0, h0 + HH)
+            rope_add(nc.gpsimd, 1, h0, h0 + HH)
+        rope_turned(2, 0, HEADS)
+        rope_straight(2, 0, HH)
+        rope_straight(2, HH, HEADS)
+        rope_turned(3, 0, HEADS)
+        rope_add(nc.vector, 2, 0, HH)
+        rope_add(nc.vector, 2, HH, HEADS)
         scale_heads(1, 0, HH)
         store(1, 0, HH)
         sum_squares(3, 0, HH)
@@ -285,16 +290,16 @@ def tile_rawkvinjector_pa_s_kernel(
         store(2, 0, HH)
         scale_heads(2, HH, HEADS)
         store(2, HH, HEADS)
-        rope_turned(3, 0, HEADS)
         rope_straight(3, 0, HH)
         rope_straight(3, HH, HEADS)
-        for h0 in (0, HH):
-            rope_add(nc.vector, 3, h0, h0 + HH)
-        for h0 in (0, HH):
-            nc.vector.tensor_tensor(
-                out=result[3][:, h0 : h0 + HH, :],
-                in0=normed[3][:, h0 : h0 + HH, :],
-                in1=rstd[3][:, h0 : h0 + HH].unsqueeze(2).to_broadcast([P, HH, HD]),
-                op=ALU.mult,
-            )
-            store(3, h0, h0 + HH)
+        rope_add(nc.vector, 3, 0, HH)
+        scale_heads(3, 0, HH)
+        store(3, 0, HH)
+        rope_add(nc.vector, 3, HH, HEADS)
+        nc.vector.tensor_tensor(
+            out=result[3][:, HH:HEADS, :],
+            in0=normed[3][:, HH:HEADS, :],
+            in1=rstd[3][:, HH:HEADS].unsqueeze(2).to_broadcast([P, HH, HD]),
+            op=ALU.mult,
+        )
+        store(3, HH, HEADS)

@@ -274,10 +274,14 @@ def tile_rawkvinjector_pa_s_kernel(
             rope_add(nc.gpsimd, 1, h0, h0 + HH)
         rope_turned(2, 0, HEADS)
         rope_straight(2, 0, HH)
+        rope_add(nc.gpsimd, 2, 0, HH)
         rope_straight(2, HH, HEADS)
         rope_turned(3, 0, HEADS)
-        rope_add(nc.vector, 2, 0, HH)
+        rope_straight(3, 0, HH)
+        rope_straight(3, HH, HEADS)
         rope_add(nc.vector, 2, HH, HEADS)
+        rope_add(nc.vector, 3, HH, HEADS)
+        rope_add(nc.vector, 3, 0, HH)
         scale_heads(1, 0, HH)
         store(1, 0, HH)
         sum_squares(3, 0, HH)
@@ -286,20 +290,6 @@ def tile_rawkvinjector_pa_s_kernel(
         sum_squares(3, HH, HEADS)
         inverse_rms(2)
         inverse_rms(3)
-        scale_heads(2, 0, HH)
-        store(2, 0, HH)
-        scale_heads(2, HH, HEADS)
-        store(2, HH, HEADS)
-        rope_straight(3, 0, HH)
-        rope_straight(3, HH, HEADS)
-        rope_add(nc.vector, 3, 0, HH)
-        scale_heads(3, 0, HH)
-        store(3, 0, HH)
-        rope_add(nc.vector, 3, HH, HEADS)
-        nc.vector.tensor_tensor(
-            out=result[3][:, HH:HEADS, :],
-            in0=normed[3][:, HH:HEADS, :],
-            in1=rstd[3][:, HH:HEADS].unsqueeze(2).to_broadcast([P, HH, HD]),
-            op=ALU.mult,
-        )
-        store(3, HH, HEADS)
+        for c, h0 in ((2, 0), (2, HH), (3, HH), (3, 0)):
+            scale_heads(c, h0, h0 + HH)
+            store(c, h0, h0 + HH)

@@ -268,28 +268,26 @@ def tile_rawkvinjector_pa_s_kernel(
         store(V_CHUNK, 0, HEADS)
         inverse_rms(1)
         sum_squares(2, 0, HEADS)
+        sum_squares(3, 0, HH)
+        inverse_rms(2)
         for h0 in (0, HH):
             rope_turned(1, h0, h0 + HH)
             rope_straight(1, h0, h0 + HH)
             rope_add(nc.gpsimd, 1, h0, h0 + HH)
+            scale_heads(1, h0, h0 + HH)
+            store(1, h0, h0 + HH)
         rope_turned(2, 0, HEADS)
         rope_straight(2, 0, HH)
         rope_add(nc.gpsimd, 2, 0, HH)
         rope_straight(2, HH, HEADS)
+        sum_squares(3, HH, HEADS)
+        scale_heads(2, 0, HH)
+        store(2, 0, HH)
+        inverse_rms(3)
         rope_turned(3, 0, HEADS)
         rope_straight(3, 0, HH)
         rope_straight(3, HH, HEADS)
-        rope_add(nc.vector, 2, HH, HEADS)
-        rope_add(nc.vector, 3, HH, HEADS)
-        rope_add(nc.vector, 3, 0, HH)
-        scale_heads(1, 0, HH)
-        store(1, 0, HH)
-        sum_squares(3, 0, HH)
-        scale_heads(1, HH, HEADS)
-        store(1, HH, HEADS)
-        sum_squares(3, HH, HEADS)
-        inverse_rms(2)
-        inverse_rms(3)
-        for c, h0 in ((2, 0), (2, HH), (3, HH), (3, 0)):
+        for c, h0 in ((2, HH), (3, HH), (3, 0)):
+            rope_add(nc.vector, c, h0, h0 + HH)
             scale_heads(c, h0, h0 + HH)
             store(c, h0, h0 + HH)

@@ -17,7 +17,7 @@ HALF = HD // 2
 CHUNK = 512
 HEADS = CHUNK // HD
 EPS = 1e-6
-SCALAR_COLS = 256
+SCALAR_COLS = 248
 
 FLOPS = 2 * P * D * 4 * CHUNK
 

import concourse.mybir as mybir
from concourse.masks import make_identity

F32 = mybir.dt.float32
BF16 = mybir.dt.bfloat16
U32 = mybir.dt.uint32
U8 = mybir.dt.uint8
FP8X4 = mybir.dt.float8_e4m3fn_x4
ALU = mybir.AluOpType
ACT = mybir.ActivationFunctionType

P = 128
PACK = 4
D = P * PACK
HD = 64
HALF = HD // 2
CHUNK = 512
HEADS = CHUNK // HD
EPS = 1e-6
SCALAR_COLS = 248

FLOPS = 2 * P * D * 4 * CHUNK


def tile_rawkvinjector_pa_s_kernel(
    tc, hidden_states, ln1_w, Wq, Wk, Wv, q_norm_w, k_norm_w, cos, sin, out_0, out_1, out_2
):
    nc = tc.nc
    vector_cols = (0, CHUNK - SCALAR_COLS)
    scalar_cols = (CHUNK - SCALAR_COLS, CHUNK)
    V_CHUNK = 0
    chunks = [
        (Wv, 0, out_2, 0, None),
        (Wk, 0, out_1, 0, 1),
        (Wq, 0, out_0, 0, 0),
        (Wq, CHUNK, out_0, HEADS, 0),
    ]
    every = range(4)
    normed_chunks = range(1, 4)
    with (
        nc.allow_non_contiguous_dma(reason="outputs are stored head by head, 256 bytes a run"),
        tc.tile_pool(name="keep", bufs=1) as keep,
        tc.psum_pool(name="psum", bufs=1) as psum,
        tc.manual_schedule(),
    ):
        raw = [keep.tile([P, PACK, CHUNK], BF16, name="raw%d" % c) for c in every]
        grouped = [
            keep.tile([P, CHUNK, PACK], BF16, name="grouped%d" % c, align_bytes=64) for c in every
        ]
        codes = [keep.tile([P, CHUNK], U32, name="codes%d" % c, align_bytes=64) for c in every]
        scales = [keep.tile([P, CHUNK], U8, name="scales%d" % c, align_bytes=64) for c in every]
        ln_rows = psum.tile([P, PACK, P], F32, name="ln_rows", tag="prod3")
        prod = [psum.tile([P, HEADS, HD], F32, name="prod%d" % c, tag="prod%d" % c) for c in range(2)]
        prod_sq = {c: psum.tile([P, HEADS, HD], F32, name="prod_sq%d" % c) for c in normed_chunks}
        result = [keep.tile([P, HEADS, HD], F32, name="result%d" % c) for c in every]
        squares = {c: keep.tile([P, HEADS, HD], F32, name="squares%d" % c) for c in normed_chunks}
        ssq = {c: keep.tile([P, HEADS], F32, name="ssq%d" % c) for c in normed_chunks}
        rstd = {c: keep.tile([P, HEADS], F32, name="rstd%d" % c) for c in normed_chunks}
        normed = {c: keep.tile([P, HEADS, HD], F32, name="normed%d" % c) for c in normed_chunks}
        turned = {c: keep.tile([P, HEADS, HD], F32, name="turned%d" % c) for c in normed_chunks}
        h_codes = keep.tile([P, P], U32, align_bytes=64)
        h_scales = keep.tile([P, P], U8, align_bytes=64)
        tables = keep.tile([P, 2, 2, HD], F32)
        rope_cos = tables[:, 0, :, :]
        rope_sin = tables[:, 1, :, :]

        def load(c):
            w, col0 = chunks[c][0], chunks[c][1]
            nc.sync.dma_start(
                out=raw[c][:],
                in_=w.rearrange("(p j) n -> p j n", j=PACK)[:, :, col0 : col0 + CHUNK],
            )

        def regroup(copy, c, cols):
            lo, hi = cols
            copy(
                out=grouped[c][:, lo:hi, :].rearrange("p (n i) j -> p n j i", i=4),
                in_=raw[c][:, :, lo:hi].rearrange("p j (n i) -> p n j i", i=4),
            )

        def quantise_and_multiply(c):
            nc.vector.quantize_mx(
                out=codes[c][:].bitcast(FP8X4),
                scales=scales[c][:],
                in_=grouped[c][:].rearrange("p n j -> p (n j)"),
            )
            for bank in (prod[c],) if c == V_CHUNK else (prod_sq[c], prod[c]):
                nc.tensor.matmul_mx(
                    out=bank[:].rearrange("p h d -> p (h d)"),
                    lhsT=h_codes[:].bitcast(FP8X4),
                    lhsT_scale=h_scales[:],
                    rhs=codes[c][:].bitcast(FP8X4),
                    rhs_scale=scales[c][:],
                    start=True,
                    stop=True,
                )

        def copy_v(h0, h1):
            nc.scalar.copy(out=result[V_CHUNK][:, h0:h1, :], in_=prod[V_CHUNK][:, h0:h1, :])

        def sum_squares(c, h0, h1):
            for h in range(h0, h1):
                nc.scalar.activation(
                    out=squares[c][:, h, :],
                    in_=prod_sq[c][:, h, :],
                    func=ACT.Square,
                    accum_out=ssq[c][:, h : h + 1],
                )

        def inverse_rms(c):
            nc.scalar.activation(
                out=rstd[c][:],
                in_=ssq[c][:],
                func=ACT.Abs_reciprocal_sqrt,
                scale=1.0 / HD,
                bias=EPS,
            )

        def rope_turned(c, h0, h1):
            norm = chunks[c][4]
            n = h1 - h0
            nc.vector.tensor_tensor(
                out=turned[c][:, h0:h1, 0:HALF],
                in0=prod[c][:, h0:h1, HALF:HD],
                in1=rope_sin[:, norm, 0:HALF].unsqueeze(1).to_broadcast([P, n, HALF]),
                op=ALU.mult,
            )
            nc.vector.tensor_tensor(
                out=turned[c][:, h0:h1, HALF:HD],
                in0=prod[c][:, h0:h1, 0:HALF],
                in1=rope_sin[:, norm, HALF:HD].unsqueeze(1).to_broadcast([P, n, HALF]),
                op=ALU.mult,
            )

        def rope_straight(c, h0, h1):
            norm = chunks[c][4]
            n = h1 - h0
            nc.vector.tensor_tensor(
                out=normed[c][:, h0:h1, :],
                in0=prod[c][:, h0:h1, :],
                in1=rope_cos[:, norm, :].unsqueeze(1).to_broadcast([P, n, HD]),
                op=ALU.mult,
            )

        def rope_add(engine, c, h0, h1):
            engine.tensor_tensor(
                out=normed[c][:, h0:h1, :],
                in0=normed[c][:, h0:h1, :],
                in1=turned[c][:, h0:h1, :],
                op=ALU.add,
            )

        def scale_heads(c, h0, h1):
            for h in range(h0, h1):
                nc.scalar.activation(
                    out=result[c][:, h, :],
                    in_=normed[c][:, h, :],
                    func=ACT.Copy,
                    scale=rstd[c][:, h : h + 1],
                )

        def store(c, h0, h1):
            out, head0 = chunks[c][2], chunks[c][3]
            nc.sync.dma_start(
                out=out.rearrange("b h t d -> t (b h) d")[:, head0 + h0 : head0 + h1, :],
                in_=result[c][:, h0:h1, :],
            )

        x = keep.tile([P, D], BF16)
        nc.sync.dma_start(out=x[:], in_=hidden_states.rearrange("b t d -> (b t) d"))
        ln_w = keep.tile([P, PACK], BF16)
        nc.sync.dma_start(out=ln_w[:], in_=ln1_w.rearrange("(p j) -> p j", j=PACK))
        load(0)
        angles = keep.tile([P, 2, HD], BF16)
        nc.sync.dma_start(out=angles[:, 0, :], in_=cos)
        nc.sync.dma_start(out=angles[:, 1, :], in_=sin)
        norm_row = keep.tile([P, 2, HD], BF16)
        nc.vector.memset(norm_row[:], 0.0)
        nc.sync.dma_start(out=norm_row[0:1, 0, :], in_=q_norm_w.unsqueeze(0))
        nc.sync.dma_start(out=norm_row[0:1, 1, :], in_=k_norm_w.unsqueeze(0))
        for c in range(1, 4):
            load(c)
        ones = keep.tile([P, P], BF16)
        nc.vector.memset(ones[:], 1.0)
        minus_ones = keep.tile([P, P], BF16)
        nc.vector.memset(minus_ones[:], -1.0)

        ident = keep.tile([P, P], F32)
        make_identity(nc, ident[:])
        ident_bf = keep.tile([P, P], BF16)
        nc.vector.tensor_copy(out=ident_bf[:], in_=ident[:])
        warm = keep.tile([P, 1], F32)
        nc.vector.memset(warm[:], 1.0)
        nc.scalar.activation(out=warm[:], in_=warm[:], func=ACT.Abs_reciprocal_sqrt)

        x_sq = keep.tile([P, D], BF16)
        x_ssq = keep.tile([P, 1], F32)
        nc.scalar.activation(out=x_sq[:], in_=x[:], func=ACT.Square, accum_out=x_ssq[:])
        x_rstd = keep.tile([P, 1], F32)
        nc.scalar.activation(
            out=x_rstd[:], in_=x_ssq[:], func=ACT.Abs_reciprocal_sqrt, scale=1.0 / D, bias=EPS
        )
        for j in range(PACK):
            nc.tensor.matmul(
                out=ln_rows[:, j, :],
                lhsT=ln_w[:, j : j + 1].to_broadcast([P, P]),
                rhs=ident_bf[:],
                start=True,
                stop=True,
            )
        h = keep.tile([P, D], BF16)
        nc.vector.scalar_tensor_tensor(
            out=h[:].rearrange("t (p j) -> t p j", j=PACK),
            in0=x[:].rearrange("t (p j) -> t p j", j=PACK),
            scalar=x_rstd[:],
            in1=ln_rows[:].rearrange("t j p -> t p j"),
            op0=ALU.mult,
            op1=ALU.mult,
        )
        norm_w = psum.tile([P, 2, 2, HD], F32, name="norm_w", tag="prod2")
        for turn, out_d, sign, in_d in (
            (0, slice(0, HD), ones, slice(0, HD)),
            (1, slice(0, HALF), minus_ones, slice(HALF, HD)),
            (1, slice(HALF, HD), ones, slice(0, HALF)),
        ):
            nc.tensor.matmul(
                out=norm_w[:, turn, :, out_d],
                lhsT=sign[:],
                rhs=norm_row[:, :, in_d],
                start=True,
                stop=True,
            )
        h_words = h[:].bitcast(F32)
        h_turned = psum.tile([P, 2, P], F32)
        for u in range(2):
            nc.tensor.transpose(h_turned[:, u, :], h_words[:, u::2], ident[:])
        regroup(nc.vector.tensor_copy, 0, vector_cols)
        nc.vector.tensor_tensor(
            out=tables[:],
            in0=norm_w[:],
            in1=angles[:].unsqueeze(2).to_broadcast([P, 2, 2, HD]),
            op=ALU.mult,
        )
        h_grouped = keep.tile([P, P, PACK], BF16, align_bytes=64)
        nc.vector.tensor_copy(
            out=h_grouped[:].bitcast(F32), in_=h_turned[:].rearrange("p u t -> p t u")
        )
        for c in (2, 3):
            prod.append(psum.tile([P, HEADS, HD], F32, name="prod%d" % c, tag="prod%d" % c))
        regroup(nc.vector.tensor_copy, 1, vector_cols)
        for c in every:
            regroup(nc.scalar.copy, c, scalar_cols)
        nc.vector.quantize_mx(
            out=h_codes[:].bitcast(FP8X4),
            scales=h_scales[:],
            in_=h_grouped[:].rearrange("p t j -> p (t j)"),
        )
        quantise_and_multiply(0)
        regroup(nc.vector.tensor_copy, 2, vector_cols)
        quantise_and_multiply(1)
        regroup(nc.vector.tensor_copy, 3, vector_cols)
        quantise_and_multiply(2)
        quantise_and_multiply(3)

        HH = HEADS // 2
        sum_squares(1, 0, HEADS)
        copy_v(0, HEADS)
        store(V_CHUNK, 0, HEADS)
        inverse_rms(1)
        sum_squares(2, 0, HEADS)
        sum_squares(3, 0, HH)
        inverse_rms(2)
        for h0 in (0, HH):
            rope_turned(1, h0, h0 + HH)
            rope_straight(1, h0, h0 + HH)
            rope_add(nc.gpsimd, 1, h0, h0 + HH)
            scale_heads(1, h0, h0 + HH)
            store(1, h0, h0 + HH)
        rope_turned(2, 0, HEADS)
        rope_straight(2, 0, HH)
        rope_add(nc.gpsimd, 2, 0, HH)
        rope_straight(2, HH, HEADS)
        sum_squares(3, HH, HEADS)
        scale_heads(2, 0, HH)
        store(2, 0, HH)
        inverse_rms(3)
        rope_turned(3, 0, HEADS)
        rope_straight(3, 0, HH)
        rope_straight(3, HH, HEADS)
        for c, h0 in ((2, HH), (3, HH), (3, 0)):
            rope_add(nc.vector, c, h0, h0 + HH)
            scale_heads(c, h0, h0 + HH)
            store(c, h0, h0 + HH)
